import numpy as np
import ml_dtypes


def mxq(x, axis, fmt="e4m3"):
    dtype, down = {"e4m3": (ml_dtypes.float8_e4m3fn, 7), "e5m2": (ml_dtypes.float8_e5m2, 14)}[fmt]
    v = np.moveaxis(np.asarray(x, np.float32).astype(ml_dtypes.bfloat16).astype(np.float64), axis, -1)
    blocks = v.reshape(v.shape[:-1] + (-1, 32))
    amax = np.abs(blocks).max(-1, keepdims=True)
    byte = np.maximum(np.where(amax > 0, np.frexp(amax)[1] - 1 + 127, 0) - down, 1)
    scale = np.exp2(byte - 127.0)
    codes = (blocks / scale).astype(np.float32).astype(dtype).astype(np.float64)
    return np.moveaxis((codes * scale).reshape(v.shape), -1, axis)


WIDE = False


def mx_kscale(k):
    if not WIDE:
        return np.ones(k)
    levels = np.array([10, -10, 5, -5, 0])
    a = np.random.permutation(np.resize(levels, k // 512 * 4)).reshape(k // 512, 4)
    idx = np.arange(k)
    return np.exp2(a[idx // 512, idx % 128 // 32])


BF16 = ml_dtypes.bfloat16


def bf(x):
    return np.asarray(x, np.float32).astype(BF16)


def f64(x):
    return np.asarray(x).astype(np.float64)


B, S, DM, H, DH, QB = 4, 2048, 256, 4, 256, 512
DI = H * DH
EPS_GN = 1e-5


def setup_inputs():
    s = mx_kscale(DI)
    h = np.random.standard_normal((B, S, H, DH)) * 0.15 + np.random.standard_normal((B, 1, H, 1)) * 0.15
    return {"h_attn": bf(h.reshape(B, S, DI)),
            "gn_w": bf((1.0 + 0.1 * np.random.standard_normal(DI)) * s),
            "gn_b": bf(0.1 * np.random.standard_normal(DI) * s),
            "W_out": bf(np.random.standard_normal((DM, DI)) / np.sqrt(DI) / s[None, :]),
            "x": bf(np.random.standard_normal((B, S, DM))),
            "skip_scale": bf(0.7 + 0.1 * np.random.standard_normal(1))}


def reference(h_attn, gn_w, gn_b, W_out, x, skip_scale):
    hg = f64(h_attn).reshape(B, S, H, DH)
    mu = hg.mean(axis=(1, 3), keepdims=True)
    var = hg.var(axis=(1, 3), keepdims=True)
    hg = (hg - mu) / np.sqrt(var + EPS_GN)
    h = hg.reshape(B, S, DI) * f64(gn_w) + f64(gn_b)
    return (mxq(h, 2, "e4m3") @ mxq(f64(W_out), 1, "e4m3").T) + f64(skip_scale) * f64(x)

@@ -1,0 +1,326 @@
+from contextlib import ExitStack
+
+import concourse.mybir as mybir
+from concourse.masks import make_identity
+
+FP8X4 = mybir.dt.float8_e4m3fn_x4
+BF16 = mybir.dt.bfloat16
+F32 = mybir.dt.float32
+U32 = mybir.dt.uint32
+U8 = mybir.dt.uint8
+ALU = mybir.AluOpType
+ACT = mybir.ActivationFunctionType
+AXIS = mybir.AxisListType
+
+P = 128
+PACK = 4
+K_PASS = P * PACK
+
+BATCH, SEQ, CHANNELS, D_MODEL = 4, 2048, 1024, 256
+GROUP = 256
+EPS = 1e-5
+
+PASSES = CHANNELS // K_PASS
+GROUPS = CHANNELS // GROUP
+C_TILES = CHANNELS // P
+TILES_PER_GROUP = GROUP // P
+QUARTERS = 4
+ROWS = SEQ // P // QUARTERS
+UNIT_TOKENS = ROWS * P
+UNITS = BATCH * QUARTERS
+H_BUFS = 12
+STATS_LEAD = 5
+
+FLOPS = 2 * BATCH * SEQ * CHANNELS * D_MODEL
+
+
+def tile_mlstmblock_pb_t_kernel(tc, h_attn, gn_w, gn_b, W_out, x, skip_scale, out):
+    nc = tc.nc
+    h_view = h_attn.rearrange("b (p q r) c -> b q p r c", q=QUARTERS, r=ROWS)
+    x_view = x.rearrange("b (p q r) d -> b p q r d", q=QUARTERS, r=ROWS)
+    out_view = out.rearrange("b (p q r) d -> b q p r d", q=QUARTERS, r=ROWS)
+
+    with ExitStack() as ctx:
+        consts = ctx.enter_context(tc.tile_pool(name="consts", bufs=1))
+        h_pool = ctx.enter_context(tc.tile_pool(name="h_pool", bufs=H_BUFS))
+        work = ctx.enter_context(tc.tile_pool(name="work", bufs=2))
+        stat_pool = ctx.enter_context(tc.tile_pool(name="stat_pool", bufs=4))
+        tp_psum = ctx.enter_context(tc.psum_pool(name="tp_psum", bufs=4))
+        mm_psum = ctx.enter_context(tc.psum_pool(name="mm_psum", bufs=2))
+        stat_psum = ctx.enter_context(tc.psum_pool(name="stat_psum", bufs=2))
+        ctx.enter_context(tc.manual_schedule())
+
+        h_tiles = {}
+        x_tiles = {}
+
+        def load_h(u):
+            b, q = divmod(u, QUARTERS)
+            h_tile = h_pool.tile([P, ROWS, CHANNELS], BF16, name="h_tile")
+            nc.sync.dma_start(out=h_tile[:], in_=h_view[b, q])
+            h_tiles[u] = h_tile
+
+        def load_x(b):
+            x_tile = work.tile([P, QUARTERS, ROWS, D_MODEL], BF16, name="x_tile")
+            nc.sync.dma_start(out=x_tile[:], in_=x_view[b])
+            x_tiles[b] = x_tile
+
+        ident = consts.tile([P, P], BF16, name="ident")
+        make_identity(nc, ident[:])
+        ones_col = consts.tile([P, 2], BF16, name="ones_col")
+        nc.vector.memset(ones_col[:], 1.0)
+        mean_mat = consts.tile([P, P], F32, name="mean_mat")
+        nc.vector.memset(mean_mat[:], 1.0 / (SEQ * GROUP))
+        gn_rows = consts.tile([P, P], BF16, name="gn_rows")
+        nc.vector.memset(gn_rows[:], 0.0)
+        warm = consts.tile([P, 1], F32, name="warm")
+        nc.vector.memset(warm[:], 1.0)
+
+        nc.sync.dma_start(out=gn_rows[0:C_TILES, :], in_=gn_w.rearrange("(c p) -> c p", p=P))
+        nc.sync.dma_start(out=gn_rows[C_TILES : 2 * C_TILES, :], in_=gn_b.rearrange("(c p) -> c p", p=P))
+        skip_bf = consts.tile([P, 1], BF16, name="skip_bf")
+        nc.sync.dma_start(out=skip_bf[:], in_=skip_scale.partition_broadcast(P))
+        nc.scalar.activation(out=warm[:], in_=warm[:], func=ACT.Sqrt)
+
+        w_raw = consts.tile([P, D_MODEL // P, CHANNELS], BF16, name="w_raw")
+        nc.sync.dma_start(out=w_raw[:], in_=W_out.rearrange("(m p) c -> p m c", p=P))
+        for u in range(QUARTERS):
+            load_h(u)
+        load_x(0)
+        for u in range(QUARTERS, H_BUFS):
+            load_h(u)
+
+        gn_ps = tp_psum.tile([P, 2 * UNIT_TOKENS], BF16, name="tp")
+        nc.tensor.transpose(gn_ps[:, 0:P], gn_rows[:], ident[:])
+        gn_cols = consts.tile([P, 2 * C_TILES], F32, name="gn_cols")
+        nc.vector.tensor_copy(out=gn_cols[:], in_=gn_ps[:, 0 : 2 * C_TILES])
+        skip_f = consts.tile([P, 1], F32, name="skip_f")
+        nc.vector.tensor_copy(out=skip_f[:], in_=skip_bf[:])
+
+        w_grouped = consts.tile([P, PASSES, D_MODEL, PACK], BF16, name="w_grouped", align_bytes=64)
+        w_codes = consts.tile([P, PASSES * D_MODEL], U32, name="w_codes", align_bytes=64)
+        w_scales = consts.tile([P, PASSES * D_MODEL], U8, name="w_scales", align_bytes=64)
+        for k in range(PASSES):
+            w_ps = tp_psum.tile([P, PACK * D_MODEL], BF16, name="tp")
+            for t in range(PACK):
+                for m in range(D_MODEL // P):
+                    c0 = k * K_PASS + t * P
+                    nc.tensor.transpose(
+                        w_ps[:, t * D_MODEL + m * P : t * D_MODEL + (m + 1) * P], w_raw[:, m, c0 : c0 + P], ident[:]
+                    )
+            nc.vector.tensor_copy(out=w_grouped[:, k], in_=w_ps[:].rearrange("p (t n) -> p n t", t=PACK))
+        nc.vector.quantize_mx(
+            out=w_codes[:].bitcast(FP8X4), scales=w_scales[:], in_=w_grouped[:].rearrange("p k n t -> p (k n t)")
+        )
+
+        N_SUMS = C_TILES * QUARTERS
+        sq_parts = {}
+        stat_banks = {}
+        moments = {}
+        stds = {}
+        scale_bias = {}
+
+        def sum_squares(u, groups):
+            b, q = divmod(u, QUARTERS)
+            for g in groups:
+                if q == 0 and g % 2 == 0:
+                    sq_parts[(b, g // 2)] = stat_pool.tile([P, 2, QUARTERS], F32, name="sq_part")
+                part = sq_parts[(b, g // 2)][:, g % 2, q : q + 1]
+                src = h_tiles[u][:, :, g * GROUP : (g + 1) * GROUP]
+                if b == 0 and g >= 2:
+                    squares_v = work.tile([P, ROWS, GROUP], BF16, name="squares_v")
+                    nc.vector.scalar_tensor_tensor(
+                        out=squares_v[:], in0=src, scalar=1.0, in1=src, op0=ALU.mult, op1=ALU.mult, accum_out=part
+                    )
+                else:
+                    squares = work.tile([P, ROWS, GROUP], BF16, name="squares")
+                    nc.scalar.activation(out=squares[:], in_=src, func=ACT.Square, accum_out=part)
+
+        def sum_channels(u):
+            b, q = divmod(u, QUARTERS)
+            if q == 0:
+                stat_banks[b] = stat_psum.tile([P, 64], F32, name="stat_bank")
+            for c in range(C_TILES):
+                col = c * QUARTERS + q
+                for r in range(ROWS):
+                    nc.tensor.matmul(
+                        out=stat_banks[b][:, col : col + 1],
+                        lhsT=h_tiles[u][:, r, c * P : (c + 1) * P],
+                        rhs=ones_col[:, 0:1],
+                        start=(r == 0),
+                        stop=(r == ROWS - 1),
+                    )
+
+        def total_stats(b):
+            bank = stat_banks[b]
+            sums = stat_pool.tile([P, GROUPS], F32, name="sums")
+            nc.vector.tensor_reduce(
+                out=sums[:], in_=bank[:, 0:N_SUMS].rearrange("p (g j) -> p g j", g=GROUPS), axis=AXIS.X, op=ALU.add
+            )
+            nc.tensor.matmul(out=bank[:, N_SUMS : N_SUMS + GROUPS], lhsT=mean_mat[:], rhs=sums[:], start=True, stop=True)
+            for pair in range(GROUPS // 2):
+                lo = N_SUMS + GROUPS + 2 * pair
+                for q in range(QUARTERS):
+                    nc.tensor.matmul(
+                        out=bank[:, lo : lo + 2],
+                        lhsT=mean_mat[:],
+                        rhs=sq_parts[(b, pair)][:, :, q],
+                        start=(q == 0),
+                        stop=(q == QUARTERS - 1),
+                    )
+
+        def variance(b):
+            both = stat_pool.tile([P, 2, GROUPS], F32, name="both")
+            nc.vector.tensor_copy(
+                out=both[:].rearrange("p a g -> p (a g)"), in_=stat_banks[b][:, N_SUMS : N_SUMS + 2 * GROUPS]
+            )
+            mean_sq = stat_pool.tile([P, GROUPS], F32, name="mean_sq")
+            nc.vector.tensor_tensor(out=mean_sq[:], in0=both[:, 0, :], in1=both[:, 0, :], op=ALU.mult)
+            var_eps = stat_pool.tile([P, GROUPS], F32, name="var_eps")
+            nc.vector.scalar_tensor_tensor(
+                out=var_eps[:], in0=both[:, 1, :], scalar=EPS, in1=mean_sq[:], op0=ALU.add, op1=ALU.subtract
+            )
+            std = stat_pool.tile([P, GROUPS], F32, name="std")
+            nc.scalar.activation(out=std[:], in_=var_eps[:], func=ACT.Sqrt)
+            moments[b] = both
+            stds[b] = std
+
+        def scale_and_bias(b):
+            rstd = stat_pool.tile([P, GROUPS], F32, name="rstd")
+            nc.vector.reciprocal(out=rstd[:], in_=stds[b][:])
+            shape = [P, GROUPS, TILES_PER_GROUP]
+            w_cols = gn_cols[:, 0:C_TILES].rearrange("p (g c) -> p g c", g=GROUPS)
+            b_cols = gn_cols[:, C_TILES : 2 * C_TILES].rearrange("p (g c) -> p g c", g=GROUPS)
+            scale = stat_pool.tile(shape, F32, name="scale")
+            nc.vector.tensor_tensor(out=scale[:], in0=w_cols, in1=rstd[:].unsqueeze(2).to_broadcast(shape), op=ALU.mult)
+            shift = stat_pool.tile(shape, F32, name="shift")
+            nc.vector.tensor_tensor(
+                out=shift[:], in0=scale[:], in1=moments[b][:, 0, :].unsqueeze(2).to_broadcast(shape), op=ALU.mult
+            )
+            bias = stat_pool.tile(shape, F32, name="bias")
+            nc.vector.tensor_tensor(out=bias[:], in0=b_cols, in1=shift[:], op=ALU.subtract)
+            scale_bias[b] = (scale[:].rearrange("p g c -> p (g c)"), bias[:].rearrange("p g c -> p (g c)"))
+
+        planes_of = {}
+        grouped_of = {}
+        codes_of = {}
+        acc_of = {}
+
+        def normalise(u):
+            scale, bias = scale_bias[u // QUARTERS]
+            planes = work.tile([P, C_TILES, UNIT_TOKENS], BF16, name="planes")
+            on_scalar = 1 + u % 2 if u + STATS_LEAD - 1 < UNITS else GROUPS
+            banks = []
+            for g in range(GROUPS):
+                tp = tp_psum.tile([P, TILES_PER_GROUP, UNIT_TOKENS], BF16, name="tp")
+                for j in range(TILES_PER_GROUP):
+                    c = g * TILES_PER_GROUP + j
+                    for r in range(ROWS):
+                        nc.tensor.transpose(tp[:, j, r * P : (r + 1) * P], h_tiles[u][:, r, c * P : (c + 1) * P], ident[:])
+                banks.append(tp)
+            for g in range(GROUPS):
+                for j in range(TILES_PER_GROUP):
+                    c = g * TILES_PER_GROUP + j
+                    if g < on_scalar:
+                        nc.scalar.activation(
+                            out=planes[:, c, :],
+                            in_=banks[g][:, j, :],
+                            func=ACT.Identity,
+                            scale=scale[:, c : c + 1],
+                            bias=bias[:, c : c + 1],
+                        )
+                    else:
+                        nc.vector.tensor_scalar(
+                            out=planes[:, c, :],
+                            in0=banks[g][:, j, :],
+                            scalar1=scale[:, c : c + 1],
+                            scalar2=bias[:, c : c + 1],
+                            op0=ALU.mult,
+                            op1=ALU.add,
+                        )
+            planes_of[u] = planes
+
+        def regroup(u):
+            grouped = work.tile([P, PASSES, UNIT_TOKENS, PACK], BF16, name="grouped", align_bytes=64)
+            for k in range(PASSES):
+                nc.vector.tensor_copy(
+                    out=grouped[:, k].rearrange("p (c i) t -> p c t i", i=4),
+                    in_=planes_of[u][:, k * PACK : (k + 1) * PACK, :].rearrange("p t (c i) -> p c t i", i=4),
+                )
+            grouped_of[u] = grouped
+
+        def quantise(u):
+            codes = work.tile([P, PASSES * UNIT_TOKENS], U32, name="codes", align_bytes=64)
+            scales = work.tile([P, PASSES * UNIT_TOKENS], U8, name="scales", align_bytes=64)
+            nc.vector.quantize_mx(
+                out=codes[:].bitcast(FP8X4), scales=scales[:], in_=grouped_of[u][:].rearrange("p k r t -> p (k r t)")
+            )
+            codes_of[u] = (codes, scales)
+
+        def multiply(u):
+            codes, scales = codes_of[u]
+            acc_of[u] = []
+            for pair in range(ROWS // 2):
+                acc = mm_psum.tile([P, 2, D_MODEL], F32, name="acc")
+                for s in range(2):
+                    for k in range(PASSES):
+                        lo = k * UNIT_TOKENS + (2 * pair + s) * P
+                        nc.tensor.matmul_mx(
+                            out=acc[:, s, :],
+                            lhsT=codes[:, lo : lo + P].bitcast(FP8X4),
+                            lhsT_scale=scales[:, lo : lo + P],
+                            rhs=w_codes[:, k * D_MODEL : (k + 1) * D_MODEL].bitcast(FP8X4),
+                            rhs_scale=w_scales[:, k * D_MODEL : (k + 1) * D_MODEL],
+                            start=(k == 0),
+                            stop=(k == PASSES - 1),
+                        )
+                acc_of[u].append(acc)
+
+        def add_skip_and_store(u):
+            b, q = divmod(u, QUARTERS)
+            result = work.tile([P, ROWS, D_MODEL], F32, name="result")
+            for pair in range(ROWS // 2):
+                nc.vector.scalar_tensor_tensor(
+                    out=result[:, 2 * pair : 2 * pair + 2, :].rearrange("p s d -> p (s d)"),
+                    in0=x_tiles[b][:, q, 2 * pair : 2 * pair + 2, :].rearrange("p s d -> p (s d)"),
+                    scalar=skip_f[:, 0:1],
+                    in1=acc_of[u][pair][:].rearrange("p s d -> p (s d)"),
+                    op0=ALU.mult,
+                    op1=ALU.add,
+                )
+            nc.sync.dma_start(out=out_view[b, q], in_=result[:])
+
+        for u in range(QUARTERS):
+            sum_squares(u, range(GROUPS))
+            sum_channels(u)
+        total_stats(0)
+        variance(0)
+        scale_and_bias(0)
+
+        for i in range(-1, UNITS + 1):
+            ahead = i + STATS_LEAD
+            new_batch = (i + 1) % QUARTERS == 0 and 0 < i + 1 < UNITS
+            if 0 <= i - 1:
+                multiply(i - 1)
+            if 0 <= i < UNITS:
+                regroup(i)
+            if ahead < UNITS:
+                sum_squares(ahead, (0, 1))
+            if new_batch:
+                variance((i + 1) // QUARTERS)
+            if 0 <= i - 1:
+                add_skip_and_store(i - 1)
+            if 0 <= i and i % QUARTERS == 0 and i // QUARTERS + 1 < BATCH:
+                load_x(i // QUARTERS + 1)
+            if new_batch:
+                scale_and_bias((i + 1) // QUARTERS)
+            if i + 1 < UNITS:
+                normalise(i + 1)
+                if i + 1 + H_BUFS < UNITS:
+                    load_h(i + 1 + H_BUFS)
+            if 0 <= i < UNITS:
+                quantise(i)
+            if ahead < UNITS:
+                sum_squares(ahead, (2, 3))
+                sum_channels(ahead)
+                if ahead % QUARTERS == QUARTERS - 1:
+                    total_stats(ahead // QUARTERS)

@@ -10,7 +10,6 @@ U32 = mybir.dt.uint32
 U8 = mybir.dt.uint8
 ALU = mybir.AluOpType
 ACT = mybir.ActivationFunctionType
-AXIS = mybir.AxisListType
 
 P = 128
 PACK = 4
@@ -21,48 +20,48 @@ GROUP = 256
 EPS = 1e-5
 
 PASSES = CHANNELS // K_PASS
-GROUPS = CHANNELS // GROUP
-C_TILES = CHANNELS // P
+GROUPS_PER_PASS = K_PASS // GROUP
 TILES_PER_GROUP = GROUP // P
-QUARTERS = 4
-ROWS = SEQ // P // QUARTERS
-UNIT_TOKENS = ROWS * P
-UNITS = BATCH * QUARTERS
-H_BUFS = 12
-STATS_LEAD = 5
+ROWS = SEQ // P
+HALVES = 2
+HALF_ROWS = ROWS // HALVES
+HALF_TOKENS = HALF_ROWS * P
 
 FLOPS = 2 * BATCH * SEQ * CHANNELS * D_MODEL
 
 
 def tile_mlstmblock_pb_t_kernel(tc, h_attn, gn_w, gn_b, W_out, x, skip_scale, out):
     nc = tc.nc
-    h_view = h_attn.rearrange("b (p q r) c -> b q p r c", q=QUARTERS, r=ROWS)
-    x_view = x.rearrange("b (p q r) d -> b p q r d", q=QUARTERS, r=ROWS)
-    out_view = out.rearrange("b (p q r) d -> b q p r d", q=QUARTERS, r=ROWS)
+    h_view = h_attn.rearrange("b (p r) c -> b p r c", r=ROWS)
+    x_view = x.rearrange("b (p r) d -> b p r d", r=ROWS)
+    out_view = out.rearrange("b (p r) d -> b p r d", r=ROWS)
 
     with ExitStack() as ctx:
         consts = ctx.enter_context(tc.tile_pool(name="consts", bufs=1))
-        h_pool = ctx.enter_context(tc.tile_pool(name="h_pool", bufs=H_BUFS))
+        h_pool = ctx.enter_context(tc.tile_pool(name="h_pool", bufs=12))
+        x_pool = ctx.enter_context(tc.tile_pool(name="x_pool", bufs=3))
         work = ctx.enter_context(tc.tile_pool(name="work", bufs=2))
-        stat_pool = ctx.enter_context(tc.tile_pool(name="stat_pool", bufs=4))
+        codes_pool = ctx.enter_context(tc.tile_pool(name="codes_pool", bufs=1))
+        stat_pool = ctx.enter_context(tc.tile_pool(name="stat_pool", bufs=3))
         tp_psum = ctx.enter_context(tc.psum_pool(name="tp_psum", bufs=4))
         mm_psum = ctx.enter_context(tc.psum_pool(name="mm_psum", bufs=2))
         stat_psum = ctx.enter_context(tc.psum_pool(name="stat_psum", bufs=2))
-        ctx.enter_context(tc.manual_schedule())
 
         h_tiles = {}
         x_tiles = {}
 
-        def load_h(u):
-            b, q = divmod(u, QUARTERS)
-            h_tile = h_pool.tile([P, ROWS, CHANNELS], BF16, name="h_tile")
-            nc.sync.dma_start(out=h_tile[:], in_=h_view[b, q])
-            h_tiles[u] = h_tile
+        def load_h(b, k, half):
+            h_tile = h_pool.tile([P, HALF_ROWS, K_PASS], BF16, name="h_tile")
+            nc.sync.dma_start(
+                out=h_tile[:],
+                in_=h_view[b, :, half * HALF_ROWS : (half + 1) * HALF_ROWS, k * K_PASS : (k + 1) * K_PASS],
+            )
+            h_tiles[(b, k, half)] = h_tile
 
-        def load_x(b):
-            x_tile = work.tile([P, QUARTERS, ROWS, D_MODEL], BF16, name="x_tile")
-            nc.sync.dma_start(out=x_tile[:], in_=x_view[b])
-            x_tiles[b] = x_tile
+        def load_x(b, half):
+            x_tile = x_pool.tile([P, HALF_ROWS, D_MODEL], BF16, name="x_tile")
+            nc.sync.dma_start(out=x_tile[:], in_=x_view[b, :, half * HALF_ROWS : (half + 1) * HALF_ROWS, :])
+            x_tiles[(b, half)] = x_tile
 
         ident = consts.tile([P, P], BF16, name="ident")
         make_identity(nc, ident[:])
@@ -70,257 +69,212 @@ def tile_mlstmblock_pb_t_kernel(tc, h_attn, gn_w, gn_b, W_out, x, skip_scale, ou
         nc.vector.memset(ones_col[:], 1.0)
         mean_mat = consts.tile([P, P], F32, name="mean_mat")
         nc.vector.memset(mean_mat[:], 1.0 / (SEQ * GROUP))
-        gn_rows = consts.tile([P, P], BF16, name="gn_rows")
-        nc.vector.memset(gn_rows[:], 0.0)
         warm = consts.tile([P, 1], F32, name="warm")
         nc.vector.memset(warm[:], 1.0)
-
-        nc.sync.dma_start(out=gn_rows[0:C_TILES, :], in_=gn_w.rearrange("(c p) -> c p", p=P))
-        nc.sync.dma_start(out=gn_rows[C_TILES : 2 * C_TILES, :], in_=gn_b.rearrange("(c p) -> c p", p=P))
-        skip_bf = consts.tile([P, 1], BF16, name="skip_bf")
-        nc.sync.dma_start(out=skip_bf[:], in_=skip_scale.partition_broadcast(P))
         nc.scalar.activation(out=warm[:], in_=warm[:], func=ACT.Sqrt)
 
+        gn_rows = consts.tile([P, P], BF16, name="gn_rows")
+        nc.vector.memset(gn_rows[:], 0.0)
+        tiles = CHANNELS // P
+        nc.scalar.dma_start(out=gn_rows[0:tiles, :], in_=gn_w.rearrange("(c p) -> c p", p=P))
+        nc.scalar.dma_start(out=gn_rows[tiles : 2 * tiles, :], in_=gn_b.rearrange("(c p) -> c p", p=P))
+        skip_bf = consts.tile([P, 1], BF16, name="skip_bf")
+        nc.scalar.dma_start(out=skip_bf[:], in_=skip_scale.partition_broadcast(P))
+
+        load_h(0, 0, 0)
+        load_h(0, 0, 1)
         w_raw = consts.tile([P, D_MODEL // P, CHANNELS], BF16, name="w_raw")
         nc.sync.dma_start(out=w_raw[:], in_=W_out.rearrange("(m p) c -> p m c", p=P))
-        for u in range(QUARTERS):
-            load_h(u)
-        load_x(0)
-        for u in range(QUARTERS, H_BUFS):
-            load_h(u)
+        load_h(0, 1, 0)
+        load_h(0, 1, 1)
+        load_x(0, 0)
+        load_x(0, 1)
+        for b in (1, 2):
+            for k in range(PASSES):
+                for half in range(HALVES):
+                    load_h(b, k, half)
 
-        gn_ps = tp_psum.tile([P, 2 * UNIT_TOKENS], BF16, name="tp")
+        gn_ps = tp_psum.tile([P, 8 * P], BF16, name="tp")
         nc.tensor.transpose(gn_ps[:, 0:P], gn_rows[:], ident[:])
-        gn_cols = consts.tile([P, 2 * C_TILES], F32, name="gn_cols")
-        nc.vector.tensor_copy(out=gn_cols[:], in_=gn_ps[:, 0 : 2 * C_TILES])
+        gn_cols = consts.tile([P, 2 * tiles], F32, name="gn_cols")
+        nc.vector.tensor_copy(out=gn_cols[:], in_=gn_ps[:, 0 : 2 * tiles])
         skip_f = consts.tile([P, 1], F32, name="skip_f")
         nc.vector.tensor_copy(out=skip_f[:], in_=skip_bf[:])
+
+        sq_parts = {}
+        stat_banks = {}
+        scale_bias = {}
+
+        def start_stats(b, k):
+            sq_parts[(b, k)] = stat_pool.tile([P, GROUPS_PER_PASS, HALVES], F32, name="sq_part")
+            stat_banks[(b, k)] = stat_psum.tile([P, 16], F32, name="stat_bank")
+
+        def square_sums(b, k, half):
+            for g in range(GROUPS_PER_PASS):
+                squares = work.tile([P, HALF_ROWS, GROUP], BF16, name="squares")
+                nc.scalar.activation(
+                    out=squares[:],
+                    in_=h_tiles[(b, k, half)][:, :, g * GROUP : (g + 1) * GROUP],
+                    func=ACT.Square,
+                    accum_out=sq_parts[(b, k)][:, g, half : half + 1],
+                )
+
+        def channel_sums(b, k, half):
+            for t in range(PACK):
+                col = t * HALVES + half
+                for r in range(HALF_ROWS):
+                    nc.tensor.matmul(
+                        out=stat_banks[(b, k)][:, col : col + 1],
+                        lhsT=h_tiles[(b, k, half)][:, r, t * P : (t + 1) * P],
+                        rhs=ones_col[:, 0:1],
+                        start=(r == 0),
+                        stop=(r == HALF_ROWS - 1),
+                    )
+
+        def finish_stats(b, k):
+            bank = stat_banks[(b, k)]
+            n_sum = PACK * HALVES
+            per_group = n_sum // GROUPS_PER_PASS
+            sums = stat_pool.tile([P, GROUPS_PER_PASS, per_group], F32, name="sums")
+            nc.vector.tensor_copy(out=sums[:].rearrange("p g j -> p (g j)"), in_=bank[:, 0:n_sum])
+            mean = bank[:, n_sum : n_sum + GROUPS_PER_PASS]
+            ex2 = bank[:, n_sum + GROUPS_PER_PASS : n_sum + 2 * GROUPS_PER_PASS]
+            for j in range(per_group):
+                nc.tensor.matmul(out=mean, lhsT=mean_mat[:], rhs=sums[:, :, j], start=(j == 0), stop=(j == per_group - 1))
+            for half in range(HALVES):
+                nc.tensor.matmul(
+                    out=ex2, lhsT=mean_mat[:], rhs=sq_parts[(b, k)][:, :, half], start=(half == 0), stop=(half == HALVES - 1)
+                )
+            mean_sq = stat_pool.tile([P, GROUPS_PER_PASS], F32, name="mean_sq")
+            nc.scalar.activation(out=mean_sq[:], in_=mean, func=ACT.Square)
+            var_eps = stat_pool.tile([P, GROUPS_PER_PASS], F32, name="var_eps")
+            nc.vector.scalar_tensor_tensor(
+                out=var_eps[:], in0=ex2, scalar=EPS, in1=mean_sq[:], op0=ALU.add, op1=ALU.subtract
+            )
+            std = stat_pool.tile([P, GROUPS_PER_PASS], F32, name="std")
+            nc.scalar.activation(out=std[:], in_=var_eps[:], func=ACT.Sqrt)
+            rstd = stat_pool.tile([P, GROUPS_PER_PASS], F32, name="rstd")
+            nc.vector.reciprocal(out=rstd[:], in_=std[:])
+            shape = [P, GROUPS_PER_PASS, TILES_PER_GROUP]
+            w_cols = gn_cols[:, k * PACK : (k + 1) * PACK].rearrange("p (g c) -> p g c", g=GROUPS_PER_PASS)
+            b_cols = gn_cols[:, tiles + k * PACK : tiles + (k + 1) * PACK].rearrange("p (g c) -> p g c", g=GROUPS_PER_PASS)
+            scale = stat_pool.tile(shape, F32, name="scale")
+            nc.vector.tensor_tensor(out=scale[:], in0=w_cols, in1=rstd[:].unsqueeze(2).to_broadcast(shape), op=ALU.mult)
+            shift = stat_pool.tile(shape, F32, name="shift")
+            nc.vector.tensor_tensor(out=shift[:], in0=scale[:], in1=mean.unsqueeze(2).to_broadcast(shape), op=ALU.mult)
+            bias = stat_pool.tile(shape, F32, name="bias")
+            nc.vector.tensor_tensor(out=bias[:], in0=b_cols, in1=shift[:], op=ALU.subtract)
+            scale_bias[(b, k)] = (scale[:].rearrange("p g c -> p (g c)"), bias[:].rearrange("p g c -> p (g c)"))
 
         w_grouped = consts.tile([P, PASSES, D_MODEL, PACK], BF16, name="w_grouped", align_bytes=64)
         w_codes = consts.tile([P, PASSES * D_MODEL], U32, name="w_codes", align_bytes=64)
         w_scales = consts.tile([P, PASSES * D_MODEL], U8, name="w_scales", align_bytes=64)
-        for k in range(PASSES):
-            w_ps = tp_psum.tile([P, PACK * D_MODEL], BF16, name="tp")
+
+        def prepare_w():
+            for k in range(PASSES):
+                w_ps = tp_psum.tile([P, PACK * D_MODEL], BF16, name="tp")
+                for t in range(PACK):
+                    for m in range(D_MODEL // P):
+                        c0 = k * K_PASS + t * P
+                        nc.tensor.transpose(
+                            w_ps[:, t * D_MODEL + m * P : t * D_MODEL + (m + 1) * P], w_raw[:, m, c0 : c0 + P], ident[:]
+                        )
+                nc.vector.tensor_copy(out=w_grouped[:, k], in_=w_ps[:].rearrange("p (t n) -> p n t", t=PACK))
+            nc.vector.quantize_mx(
+                out=w_codes[:].bitcast(FP8X4),
+                scales=w_scales[:],
+                in_=w_grouped[:].rearrange("p k n t -> p (k n t)"),
+            )
+
+        h_codes = {}
+
+        def normalise(b, k, half):
+            scale, bias = scale_bias[(b, k)]
+            planes = work.tile([P, PACK, HALF_TOKENS], BF16, name="planes")
+            on_scalar = 1 + half
             for t in range(PACK):
-                for m in range(D_MODEL // P):
-                    c0 = k * K_PASS + t * P
-                    nc.tensor.transpose(
-                        w_ps[:, t * D_MODEL + m * P : t * D_MODEL + (m + 1) * P], w_raw[:, m, c0 : c0 + P], ident[:]
-                    )
-            nc.vector.tensor_copy(out=w_grouped[:, k], in_=w_ps[:].rearrange("p (t n) -> p n t", t=PACK))
-        nc.vector.quantize_mx(
-            out=w_codes[:].bitcast(FP8X4), scales=w_scales[:], in_=w_grouped[:].rearrange("p k n t -> p (k n t)")
-        )
-
-        N_SUMS = C_TILES * QUARTERS
-        sq_parts = {}
-        stat_banks = {}
-        moments = {}
-        stds = {}
-        scale_bias = {}
-
-        def sum_squares(u, groups):
-            b, q = divmod(u, QUARTERS)
-            for g in groups:
-                if q == 0 and g % 2 == 0:
-                    sq_parts[(b, g // 2)] = stat_pool.tile([P, 2, QUARTERS], F32, name="sq_part")
-                part = sq_parts[(b, g // 2)][:, g % 2, q : q + 1]
-                src = h_tiles[u][:, :, g * GROUP : (g + 1) * GROUP]
-                if b == 0 and g >= 2:
-                    squares_v = work.tile([P, ROWS, GROUP], BF16, name="squares_v")
-                    nc.vector.scalar_tensor_tensor(
-                        out=squares_v[:], in0=src, scalar=1.0, in1=src, op0=ALU.mult, op1=ALU.mult, accum_out=part
+                tp = tp_psum.tile([P, HALF_TOKENS], BF16, name="tp")
+                for r in range(HALF_ROWS):
+                    nc.tensor.transpose(tp[:, r * P : (r + 1) * P], h_tiles[(b, k, half)][:, r, t * P : (t + 1) * P], ident[:])
+                if t >= PACK - on_scalar:
+                    nc.scalar.activation(
+                        out=planes[:, t, :], in_=tp[:], func=ACT.Identity, scale=scale[:, t : t + 1], bias=bias[:, t : t + 1]
                     )
                 else:
-                    squares = work.tile([P, ROWS, GROUP], BF16, name="squares")
-                    nc.scalar.activation(out=squares[:], in_=src, func=ACT.Square, accum_out=part)
-
-        def sum_channels(u):
-            b, q = divmod(u, QUARTERS)
-            if q == 0:
-                stat_banks[b] = stat_psum.tile([P, 64], F32, name="stat_bank")
-            for c in range(C_TILES):
-                col = c * QUARTERS + q
-                for r in range(ROWS):
-                    nc.tensor.matmul(
-                        out=stat_banks[b][:, col : col + 1],
-                        lhsT=h_tiles[u][:, r, c * P : (c + 1) * P],
-                        rhs=ones_col[:, 0:1],
-                        start=(r == 0),
-                        stop=(r == ROWS - 1),
+                    nc.vector.tensor_scalar(
+                        out=planes[:, t, :],
+                        in0=tp[:],
+                        scalar1=scale[:, t : t + 1],
+                        scalar2=bias[:, t : t + 1],
+                        op0=ALU.mult,
+                        op1=ALU.add,
                     )
+            return planes
 
-        def total_stats(b):
-            bank = stat_banks[b]
-            sums = stat_pool.tile([P, GROUPS], F32, name="sums")
-            nc.vector.tensor_reduce(
-                out=sums[:], in_=bank[:, 0:N_SUMS].rearrange("p (g j) -> p g j", g=GROUPS), axis=AXIS.X, op=ALU.add
-            )
-            nc.tensor.matmul(out=bank[:, N_SUMS : N_SUMS + GROUPS], lhsT=mean_mat[:], rhs=sums[:], start=True, stop=True)
-            for pair in range(GROUPS // 2):
-                lo = N_SUMS + GROUPS + 2 * pair
-                for q in range(QUARTERS):
-                    nc.tensor.matmul(
-                        out=bank[:, lo : lo + 2],
-                        lhsT=mean_mat[:],
-                        rhs=sq_parts[(b, pair)][:, :, q],
-                        start=(q == 0),
-                        stop=(q == QUARTERS - 1),
-                    )
-
-        def variance(b):
-            both = stat_pool.tile([P, 2, GROUPS], F32, name="both")
+        def quantise(b, k, half, planes):
+            grouped = work.tile([P, HALF_TOKENS, PACK], BF16, name="grouped", align_bytes=64)
             nc.vector.tensor_copy(
-                out=both[:].rearrange("p a g -> p (a g)"), in_=stat_banks[b][:, N_SUMS : N_SUMS + 2 * GROUPS]
+                out=grouped[:].rearrange("p (c i) t -> p c t i", i=4),
+                in_=planes[:].rearrange("p t (c i) -> p c t i", i=4),
             )
-            mean_sq = stat_pool.tile([P, GROUPS], F32, name="mean_sq")
-            nc.vector.tensor_tensor(out=mean_sq[:], in0=both[:, 0, :], in1=both[:, 0, :], op=ALU.mult)
-            var_eps = stat_pool.tile([P, GROUPS], F32, name="var_eps")
-            nc.vector.scalar_tensor_tensor(
-                out=var_eps[:], in0=both[:, 1, :], scalar=EPS, in1=mean_sq[:], op0=ALU.add, op1=ALU.subtract
-            )
-            std = stat_pool.tile([P, GROUPS], F32, name="std")
-            nc.scalar.activation(out=std[:], in_=var_eps[:], func=ACT.Sqrt)
-            moments[b] = both
-            stds[b] = std
-
-        def scale_and_bias(b):
-            rstd = stat_pool.tile([P, GROUPS], F32, name="rstd")
-            nc.vector.reciprocal(out=rstd[:], in_=stds[b][:])
-            shape = [P, GROUPS, TILES_PER_GROUP]
-            w_cols = gn_cols[:, 0:C_TILES].rearrange("p (g c) -> p g c", g=GROUPS)
-            b_cols = gn_cols[:, C_TILES : 2 * C_TILES].rearrange("p (g c) -> p g c", g=GROUPS)
-            scale = stat_pool.tile(shape, F32, name="scale")
-            nc.vector.tensor_tensor(out=scale[:], in0=w_cols, in1=rstd[:].unsqueeze(2).to_broadcast(shape), op=ALU.mult)
-            shift = stat_pool.tile(shape, F32, name="shift")
-            nc.vector.tensor_tensor(
-                out=shift[:], in0=scale[:], in1=moments[b][:, 0, :].unsqueeze(2).to_broadcast(shape), op=ALU.mult
-            )
-            bias = stat_pool.tile(shape, F32, name="bias")
-            nc.vector.tensor_tensor(out=bias[:], in0=b_cols, in1=shift[:], op=ALU.subtract)
-            scale_bias[b] = (scale[:].rearrange("p g c -> p (g c)"), bias[:].rearrange("p g c -> p (g c)"))
-
-        planes_of = {}
-        grouped_of = {}
-        codes_of = {}
-        acc_of = {}
-
-        def normalise(u):
-            scale, bias = scale_bias[u // QUARTERS]
-            planes = work.tile([P, C_TILES, UNIT_TOKENS], BF16, name="planes")
-            on_scalar = 1 + u % 2 if u + STATS_LEAD - 1 < UNITS else GROUPS
-            banks = []
-            for g in range(GROUPS):
-                tp = tp_psum.tile([P, TILES_PER_GROUP, UNIT_TOKENS], BF16, name="tp")
-                for j in range(TILES_PER_GROUP):
-                    c = g * TILES_PER_GROUP + j
-                    for r in range(ROWS):
-                        nc.tensor.transpose(tp[:, j, r * P : (r + 1) * P], h_tiles[u][:, r, c * P : (c + 1) * P], ident[:])
-                banks.append(tp)
-            for g in range(GROUPS):
-                for j in range(TILES_PER_GROUP):
-                    c = g * TILES_PER_GROUP + j
-                    if g < on_scalar:
-                        nc.scalar.activation(
-                            out=planes[:, c, :],
-                            in_=banks[g][:, j, :],
-                            func=ACT.Identity,
-                            scale=scale[:, c : c + 1],
-                            bias=bias[:, c : c + 1],
-                        )
-                    else:
-                        nc.vector.tensor_scalar(
-                            out=planes[:, c, :],
-                            in0=banks[g][:, j, :],
-                            scalar1=scale[:, c : c + 1],
-                            scalar2=bias[:, c : c + 1],
-                            op0=ALU.mult,
-                            op1=ALU.add,
-                        )
-            planes_of[u] = planes
-
-        def regroup(u):
-            grouped = work.tile([P, PASSES, UNIT_TOKENS, PACK], BF16, name="grouped", align_bytes=64)
-            for k in range(PASSES):
-                nc.vector.tensor_copy(
-                    out=grouped[:, k].rearrange("p (c i) t -> p c t i", i=4),
-                    in_=planes_of[u][:, k * PACK : (k + 1) * PACK, :].rearrange("p t (c i) -> p c t i", i=4),
-                )
-            grouped_of[u] = grouped
-
-        def quantise(u):
-            codes = work.tile([P, PASSES * UNIT_TOKENS], U32, name="codes", align_bytes=64)
-            scales = work.tile([P, PASSES * UNIT_TOKENS], U8, name="scales", align_bytes=64)
+            codes = codes_pool.tile([P, HALF_TOKENS], U32, name="codes%d%d" % (k, half), align_bytes=64)
+            scales = codes_pool.tile([P, HALF_TOKENS], U8, name="scales%d%d" % (k, half), align_bytes=64)
             nc.vector.quantize_mx(
-                out=codes[:].bitcast(FP8X4), scales=scales[:], in_=grouped_of[u][:].rearrange("p k r t -> p (k r t)")
+                out=codes[:].bitcast(FP8X4), scales=scales[:], in_=grouped[:].rearrange("p r t -> p (r t)")
             )
-            codes_of[u] = (codes, scales)
+            h_codes[(k, half)] = (codes, scales)
 
-        def multiply(u):
-            codes, scales = codes_of[u]
-            acc_of[u] = []
-            for pair in range(ROWS // 2):
+        def project(b, half):
+            result = work.tile([P, HALF_ROWS, D_MODEL], F32, name="result")
+            for pair in range(HALF_ROWS // 2):
                 acc = mm_psum.tile([P, 2, D_MODEL], F32, name="acc")
                 for s in range(2):
+                    r = 2 * pair + s
                     for k in range(PASSES):
-                        lo = k * UNIT_TOKENS + (2 * pair + s) * P
+                        codes, scales = h_codes[(k, half)]
                         nc.tensor.matmul_mx(
                             out=acc[:, s, :],
-                            lhsT=codes[:, lo : lo + P].bitcast(FP8X4),
-                            lhsT_scale=scales[:, lo : lo + P],
+                            lhsT=codes[:, r * P : (r + 1) * P].bitcast(FP8X4),
+                            lhsT_scale=scales[:, r * P : (r + 1) * P],
                             rhs=w_codes[:, k * D_MODEL : (k + 1) * D_MODEL].bitcast(FP8X4),
                             rhs_scale=w_scales[:, k * D_MODEL : (k + 1) * D_MODEL],
                             start=(k == 0),
                             stop=(k == PASSES - 1),
                         )
-                acc_of[u].append(acc)
-
-        def add_skip_and_store(u):
-            b, q = divmod(u, QUARTERS)
-            result = work.tile([P, ROWS, D_MODEL], F32, name="result")
-            for pair in range(ROWS // 2):
                 nc.vector.scalar_tensor_tensor(
                     out=result[:, 2 * pair : 2 * pair + 2, :].rearrange("p s d -> p (s d)"),
-                    in0=x_tiles[b][:, q, 2 * pair : 2 * pair + 2, :].rearrange("p s d -> p (s d)"),
+                    in0=x_tiles[(b, half)][:, 2 * pair : 2 * pair + 2, :].rearrange("p s d -> p (s d)"),
                     scalar=skip_f[:, 0:1],
-                    in1=acc_of[u][pair][:].rearrange("p s d -> p (s d)"),
+                    in1=acc[:].rearrange("p s d -> p (s d)"),
                     op0=ALU.mult,
                     op1=ALU.add,
                 )
-            nc.sync.dma_start(out=out_view[b, q], in_=result[:])
+            nc.sync.dma_start(out=out_view[b, :, half * HALF_ROWS : (half + 1) * HALF_ROWS, :], in_=result[:])
 
-        for u in range(QUARTERS):
-            sum_squares(u, range(GROUPS))
-            sum_channels(u)
-        total_stats(0)
-        variance(0)
-        scale_and_bias(0)
+        for k in range(PASSES):
+            start_stats(0, k)
+            for half in range(HALVES):
+                square_sums(0, k, half)
+                channel_sums(0, k, half)
+            finish_stats(0, k)
+            if k == 0:
+                prepare_w()
 
-        for i in range(-1, UNITS + 1):
-            ahead = i + STATS_LEAD
-            new_batch = (i + 1) % QUARTERS == 0 and 0 < i + 1 < UNITS
-            if 0 <= i - 1:
-                multiply(i - 1)
-            if 0 <= i < UNITS:
-                regroup(i)
-            if ahead < UNITS:
-                sum_squares(ahead, (0, 1))
-            if new_batch:
-                variance((i + 1) // QUARTERS)
-            if 0 <= i - 1:
-                add_skip_and_store(i - 1)
-            if 0 <= i and i % QUARTERS == 0 and i // QUARTERS + 1 < BATCH:
-                load_x(i // QUARTERS + 1)
-            if new_batch:
-                scale_and_bias((i + 1) // QUARTERS)
-            if i + 1 < UNITS:
-                normalise(i + 1)
-                if i + 1 + H_BUFS < UNITS:
-                    load_h(i + 1 + H_BUFS)
-            if 0 <= i < UNITS:
-                quantise(i)
-            if ahead < UNITS:
-                sum_squares(ahead, (2, 3))
-                sum_channels(ahead)
-                if ahead % QUARTERS == QUARTERS - 1:
-                    total_stats(ahead // QUARTERS)
+        for b in range(BATCH):
+            for k in range(PASSES):
+                for half in range(HALVES):
+                    planes = normalise(b, k, half)
+                    if b + 1 < BATCH:
+                        if half == 0:
+                            start_stats(b + 1, k)
+                        square_sums(b + 1, k, half)
+                        channel_sums(b + 1, k, half)
+                    quantise(b, k, half, planes)
+                    if b + 1 < BATCH and half == HALVES - 1:
+                        finish_stats(b + 1, k)
+                    if k == PASSES - 1:
+                        project(b, half)
+                    if b + 3 < BATCH:
+                        load_h(b + 3, k, half)
+                    if b + 1 < BATCH and k == 0:
+                        load_x(b + 1, half)

@@ -27,6 +27,8 @@ HALVES = 2
 HALF_ROWS = ROWS // HALVES
 HALF_TOKENS = HALF_ROWS * P
 
+REGROUP_PARTS = 4
+
 FLOPS = 2 * BATCH * SEQ * CHANNELS * D_MODEL
 
 
@@ -41,11 +43,12 @@ def tile_mlstmblock_pb_t_kernel(tc, h_attn, gn_w, gn_b, W_out, x, skip_scale, ou
         h_pool = ctx.enter_context(tc.tile_pool(name="h_pool", bufs=12))
         x_pool = ctx.enter_context(tc.tile_pool(name="x_pool", bufs=3))
         work = ctx.enter_context(tc.tile_pool(name="work", bufs=2))
+        single = ctx.enter_context(tc.tile_pool(name="single", bufs=1))
         codes_pool = ctx.enter_context(tc.tile_pool(name="codes_pool", bufs=1))
-        stat_pool = ctx.enter_context(tc.tile_pool(name="stat_pool", bufs=3))
+        stat_pool = ctx.enter_context(tc.tile_pool(name="stat_pool", bufs=6))
         tp_psum = ctx.enter_context(tc.psum_pool(name="tp_psum", bufs=4))
         mm_psum = ctx.enter_context(tc.psum_pool(name="mm_psum", bufs=2))
-        stat_psum = ctx.enter_context(tc.psum_pool(name="stat_psum", bufs=2))
+        stat_psum = ctx.enter_context(tc.psum_pool(name="stat_psum", bufs=1))
 
         h_tiles = {}
         x_tiles = {}
@@ -76,10 +79,10 @@ def tile_mlstmblock_pb_t_kernel(tc, h_attn, gn_w, gn_b, W_out, x, skip_scale, ou
         gn_rows = consts.tile([P, P], BF16, name="gn_rows")
         nc.vector.memset(gn_rows[:], 0.0)
         tiles = CHANNELS // P
-        nc.scalar.dma_start(out=gn_rows[0:tiles, :], in_=gn_w.rearrange("(c p) -> c p", p=P))
-        nc.scalar.dma_start(out=gn_rows[tiles : 2 * tiles, :], in_=gn_b.rearrange("(c p) -> c p", p=P))
+        nc.sync.dma_start(out=gn_rows[0:tiles, :], in_=gn_w.rearrange("(c p) -> c p", p=P))
+        nc.sync.dma_start(out=gn_rows[tiles : 2 * tiles, :], in_=gn_b.rearrange("(c p) -> c p", p=P))
         skip_bf = consts.tile([P, 1], BF16, name="skip_bf")
-        nc.scalar.dma_start(out=skip_bf[:], in_=skip_scale.partition_broadcast(P))
+        nc.sync.dma_start(out=skip_bf[:], in_=skip_scale.partition_broadcast(P))
 
         load_h(0, 0, 0)
         load_h(0, 0, 1)
@@ -94,10 +97,8 @@ def tile_mlstmblock_pb_t_kernel(tc, h_attn, gn_w, gn_b, W_out, x, skip_scale, ou
                 for half in range(HALVES):
                     load_h(b, k, half)
 
-        gn_ps = tp_psum.tile([P, 8 * P], BF16, name="tp")
-        nc.tensor.transpose(gn_ps[:, 0:P], gn_rows[:], ident[:])
-        gn_cols = consts.tile([P, 2 * tiles], F32, name="gn_cols")
-        nc.vector.tensor_copy(out=gn_cols[:], in_=gn_ps[:, 0 : 2 * tiles])
+        gn_cols = stat_psum.tile([P, P], BF16, name="gn_cols")
+        nc.tensor.transpose(gn_cols[:], gn_rows[:], ident[:])
         skip_f = consts.tile([P, 1], F32, name="skip_f")
         nc.vector.tensor_copy(out=skip_f[:], in_=skip_bf[:])
 
@@ -106,18 +107,21 @@ def tile_mlstmblock_pb_t_kernel(tc, h_attn, gn_w, gn_b, W_out, x, skip_scale, ou
         scale_bias = {}
 
         def start_stats(b, k):
-            sq_parts[(b, k)] = stat_pool.tile([P, GROUPS_PER_PASS, HALVES], F32, name="sq_part")
+            for g in range(GROUPS_PER_PASS):
+                sq_parts[(b, k, g)] = stat_pool.tile([P, HALVES], F32, name="sq_part")
             stat_banks[(b, k)] = stat_psum.tile([P, 16], F32, name="stat_bank")
 
         def square_sums(b, k, half):
             for g in range(GROUPS_PER_PASS):
                 squares = work.tile([P, HALF_ROWS, GROUP], BF16, name="squares")
-                nc.scalar.activation(
-                    out=squares[:],
-                    in_=h_tiles[(b, k, half)][:, :, g * GROUP : (g + 1) * GROUP],
-                    func=ACT.Square,
-                    accum_out=sq_parts[(b, k)][:, g, half : half + 1],
-                )
+                src = h_tiles[(b, k, half)][:, :, g * GROUP : (g + 1) * GROUP]
+                part = sq_parts[(b, k, g)][:, half : half + 1]
+                if b == 0 and k == 0 and g == 1:
+                    nc.vector.scalar_tensor_tensor(
+                        out=squares[:], in0=src, scalar=1.0, in1=src, op0=ALU.mult, op1=ALU.mult, accum_out=part
+                    )
+                else:
+                    nc.scalar.activation(out=squares[:], in_=src, func=ACT.Square, accum_out=part)
 
         def channel_sums(b, k, half):
             for t in range(PACK):
@@ -141,10 +145,15 @@ def tile_mlstmblock_pb_t_kernel(tc, h_attn, gn_w, gn_b, W_out, x, skip_scale, ou
             ex2 = bank[:, n_sum + GROUPS_PER_PASS : n_sum + 2 * GROUPS_PER_PASS]
             for j in range(per_group):
                 nc.tensor.matmul(out=mean, lhsT=mean_mat[:], rhs=sums[:, :, j], start=(j == 0), stop=(j == per_group - 1))
-            for half in range(HALVES):
-                nc.tensor.matmul(
-                    out=ex2, lhsT=mean_mat[:], rhs=sq_parts[(b, k)][:, :, half], start=(half == 0), stop=(half == HALVES - 1)
-                )
+            for g in range(GROUPS_PER_PASS):
+                for half in range(HALVES):
+                    nc.tensor.matmul(
+                        out=ex2[:, g : g + 1],
+                        lhsT=mean_mat[:],
+                        rhs=sq_parts[(b, k, g)][:, half : half + 1],
+                        start=(half == 0),
+                        stop=(half == HALVES - 1),
+                    )
             mean_sq = stat_pool.tile([P, GROUPS_PER_PASS], F32, name="mean_sq")
             nc.scalar.activation(out=mean_sq[:], in_=mean, func=ACT.Square)
             var_eps = stat_pool.tile([P, GROUPS_PER_PASS], F32, name="var_eps")
@@ -191,7 +200,7 @@ def tile_mlstmblock_pb_t_kernel(tc, h_attn, gn_w, gn_b, W_out, x, skip_scale, ou
         def normalise(b, k, half):
             scale, bias = scale_bias[(b, k)]
             planes = work.tile([P, PACK, HALF_TOKENS], BF16, name="planes")
-            on_scalar = 1 + half
+            on_scalar = 2 if b == BATCH - 1 else 0
             for t in range(PACK):
                 tp = tp_psum.tile([P, HALF_TOKENS], BF16, name="tp")
                 for r in range(HALF_ROWS):
@@ -212,11 +221,21 @@ def tile_mlstmblock_pb_t_kernel(tc, h_attn, gn_w, gn_b, W_out, x, skip_scale, ou
             return planes
 
         def quantise(b, k, half, planes):
-            grouped = work.tile([P, HALF_TOKENS, PACK], BF16, name="grouped", align_bytes=64)
-            nc.vector.tensor_copy(
-                out=grouped[:].rearrange("p (c i) t -> p c t i", i=4),
-                in_=planes[:].rearrange("p t (c i) -> p c t i", i=4),
-            )
+            grouped = single.tile([P, HALF_TOKENS, PACK], BF16, name="grouped", align_bytes=64)
+            part_tokens = HALF_TOKENS // REGROUP_PARTS
+            for part in range(REGROUP_PARTS):
+                tokens = slice(part * part_tokens, (part + 1) * part_tokens)
+                if part < REGROUP_PARTS - 1:
+                    nc.gpsimd.tensor_scalar(
+                        out=grouped[:, tokens, :],
+                        in0=planes[:, :, tokens].rearrange("p t r -> p r t"),
+                        scalar1=1.0,
+                        scalar2=0.0,
+                        op0=ALU.mult,
+                        op1=ALU.add,
+                    )
+                else:
+                    nc.scalar.copy(out=grouped[:, tokens, :], in_=planes[:, :, tokens].rearrange("p t r -> p r t"))
             codes = codes_pool.tile([P, HALF_TOKENS], U32, name="codes%d%d" % (k, half), align_bytes=64)
             scales = codes_pool.tile([P, HALF_TOKENS], U8, name="scales%d%d" % (k, half), align_bytes=64)
             nc.vector.quantize_mx(

@@ -27,8 +27,6 @@ HALVES = 2
 HALF_ROWS = ROWS // HALVES
 HALF_TOKENS = HALF_ROWS * P
 
-REGROUP_PARTS = 4
-
 FLOPS = 2 * BATCH * SEQ * CHANNELS * D_MODEL
 
 
@@ -43,12 +41,11 @@ def tile_mlstmblock_pb_t_kernel(tc, h_attn, gn_w, gn_b, W_out, x, skip_scale, ou
         h_pool = ctx.enter_context(tc.tile_pool(name="h_pool", bufs=12))
         x_pool = ctx.enter_context(tc.tile_pool(name="x_pool", bufs=3))
         work = ctx.enter_context(tc.tile_pool(name="work", bufs=2))
-        single = ctx.enter_context(tc.tile_pool(name="single", bufs=1))
         codes_pool = ctx.enter_context(tc.tile_pool(name="codes_pool", bufs=1))
         stat_pool = ctx.enter_context(tc.tile_pool(name="stat_pool", bufs=6))
         tp_psum = ctx.enter_context(tc.psum_pool(name="tp_psum", bufs=4))
         mm_psum = ctx.enter_context(tc.psum_pool(name="mm_psum", bufs=2))
-        stat_psum = ctx.enter_context(tc.psum_pool(name="stat_psum", bufs=1))
+        stat_psum = ctx.enter_context(tc.psum_pool(name="stat_psum", bufs=2))
 
         h_tiles = {}
         x_tiles = {}
@@ -97,8 +94,10 @@ def tile_mlstmblock_pb_t_kernel(tc, h_attn, gn_w, gn_b, W_out, x, skip_scale, ou
                 for half in range(HALVES):
                     load_h(b, k, half)
 
-        gn_cols = stat_psum.tile([P, P], BF16, name="gn_cols")
-        nc.tensor.transpose(gn_cols[:], gn_rows[:], ident[:])
+        gn_ps = tp_psum.tile([P, 8 * P], BF16, name="tp")
+        nc.tensor.transpose(gn_ps[:, 0:P], gn_rows[:], ident[:])
+        gn_cols = consts.tile([P, 2 * tiles], F32, name="gn_cols")
+        nc.vector.tensor_copy(out=gn_cols[:], in_=gn_ps[:, 0 : 2 * tiles])
         skip_f = consts.tile([P, 1], F32, name="skip_f")
         nc.vector.tensor_copy(out=skip_f[:], in_=skip_bf[:])
 
@@ -200,7 +199,7 @@ def tile_mlstmblock_pb_t_kernel(tc, h_attn, gn_w, gn_b, W_out, x, skip_scale, ou
         def normalise(b, k, half):
             scale, bias = scale_bias[(b, k)]
             planes = work.tile([P, PACK, HALF_TOKENS], BF16, name="planes")
-            on_scalar = 2 if b == BATCH - 1 else 0
+            on_scalar = 1 if b + 1 < BATCH else PACK - 1
             for t in range(PACK):
                 tp = tp_psum.tile([P, HALF_TOKENS], BF16, name="tp")
                 for r in range(HALF_ROWS):
@@ -221,21 +220,21 @@ def tile_mlstmblock_pb_t_kernel(tc, h_attn, gn_w, gn_b, W_out, x, skip_scale, ou
             return planes
 
         def quantise(b, k, half, planes):
-            grouped = single.tile([P, HALF_TOKENS, PACK], BF16, name="grouped", align_bytes=64)
-            part_tokens = HALF_TOKENS // REGROUP_PARTS
-            for part in range(REGROUP_PARTS):
-                tokens = slice(part * part_tokens, (part + 1) * part_tokens)
-                if part < REGROUP_PARTS - 1:
-                    nc.gpsimd.tensor_scalar(
-                        out=grouped[:, tokens, :],
-                        in0=planes[:, :, tokens].rearrange("p t r -> p r t"),
-                        scalar1=1.0,
-                        scalar2=0.0,
-                        op0=ALU.mult,
-                        op1=ALU.add,
-                    )
-                else:
-                    nc.scalar.copy(out=grouped[:, tokens, :], in_=planes[:, :, tokens].rearrange("p t r -> p r t"))
+            grouped = work.tile([P, HALF_TOKENS, PACK], BF16, name="grouped", align_bytes=64)
+            cut = HALF_TOKENS // 2
+            nc.vector.tensor_copy(
+                out=grouped[:, 0:cut, :].rearrange("p (c i) t -> p c t i", i=4),
+                in_=planes[:, :, 0:cut].rearrange("p t (c i) -> p c t i", i=4),
+            )
+            for lo in (cut, cut + cut // 2):
+                nc.gpsimd.tensor_scalar(
+                    out=grouped[:, lo : lo + cut // 2, :],
+                    in0=planes[:, :, lo : lo + cut // 2].rearrange("p t r -> p r t"),
+                    scalar1=1.0,
+                    scalar2=0.0,
+                    op0=ALU.mult,
+                    op1=ALU.add,
+                )
             codes = codes_pool.tile([P, HALF_TOKENS], U32, name="codes%d%d" % (k, half), align_bytes=64)
             scales = codes_pool.tile([P, HALF_TOKENS], U8, name="scales%d%d" % (k, half), align_bytes=64)
             nc.vector.quantize_mx(

@@ -221,15 +221,11 @@ def tile_mlstmblock_pb_t_kernel(tc, h_attn, gn_w, gn_b, W_out, x, skip_scale, ou
 
         def quantise(b, k, half, planes):
             grouped = work.tile([P, HALF_TOKENS, PACK], BF16, name="grouped", align_bytes=64)
-            cut = HALF_TOKENS // 2
-            nc.vector.tensor_copy(
-                out=grouped[:, 0:cut, :].rearrange("p (c i) t -> p c t i", i=4),
-                in_=planes[:, :, 0:cut].rearrange("p t (c i) -> p c t i", i=4),
-            )
-            for lo in (cut, cut + cut // 2):
+            piece = HALF_TOKENS // 4
+            for lo in range(0, HALF_TOKENS, piece):
                 nc.gpsimd.tensor_scalar(
-                    out=grouped[:, lo : lo + cut // 2, :],
-                    in0=planes[:, :, lo : lo + cut // 2].rearrange("p t r -> p r t"),
+                    out=grouped[:, lo : lo + piece, :],
+                    in0=planes[:, :, lo : lo + piece].rearrange("p t r -> p r t"),
                     scalar1=1.0,
                     scalar2=0.0,
                     op0=ALU.mult,

@@ -199,7 +199,7 @@ def tile_mlstmblock_pb_t_kernel(tc, h_attn, gn_w, gn_b, W_out, x, skip_scale, ou
         def normalise(b, k, half):
             scale, bias = scale_bias[(b, k)]
             planes = work.tile([P, PACK, HALF_TOKENS], BF16, name="planes")
-            on_scalar = 1 if b + 1 < BATCH else PACK - 1
+            on_scalar = 1 + half
             for t in range(PACK):
                 tp = tp_psum.tile([P, HALF_TOKENS], BF16, name="tp")
                 for r in range(HALF_ROWS):
@@ -221,16 +221,10 @@ def tile_mlstmblock_pb_t_kernel(tc, h_attn, gn_w, gn_b, W_out, x, skip_scale, ou
 
         def quantise(b, k, half, planes):
             grouped = work.tile([P, HALF_TOKENS, PACK], BF16, name="grouped", align_bytes=64)
-            piece = HALF_TOKENS // 4
-            for lo in range(0, HALF_TOKENS, piece):
-                nc.gpsimd.tensor_scalar(
-                    out=grouped[:, lo : lo + piece, :],
-                    in0=planes[:, :, lo : lo + piece].rearrange("p t r -> p r t"),
-                    scalar1=1.0,
-                    scalar2=0.0,
-                    op0=ALU.mult,
-                    op1=ALU.add,
-                )
+            nc.vector.tensor_copy(
+                out=grouped[:].rearrange("p (c i) t -> p c t i", i=4),
+                in_=planes[:].rearrange("p t (c i) -> p c t i", i=4),
+            )
             codes = codes_pool.tile([P, HALF_TOKENS], U32, name="codes%d%d" % (k, half), align_bytes=64)
             scales = codes_pool.tile([P, HALF_TOKENS], U8, name="scales%d%d" % (k, half), align_bytes=64)
             nc.vector.quantize_mx(

@@ -42,7 +42,7 @@ def tile_mlstmblock_pb_t_kernel(tc, h_attn, gn_w, gn_b, W_out, x, skip_scale, ou
         x_pool = ctx.enter_context(tc.tile_pool(name="x_pool", bufs=3))
         work = ctx.enter_context(tc.tile_pool(name="work", bufs=2))
         codes_pool = ctx.enter_context(tc.tile_pool(name="codes_pool", bufs=1))
-        stat_pool = ctx.enter_context(tc.tile_pool(name="stat_pool", bufs=6))
+        stat_pool = ctx.enter_context(tc.tile_pool(name="stat_pool", bufs=3))
         tp_psum = ctx.enter_context(tc.psum_pool(name="tp_psum", bufs=4))
         mm_psum = ctx.enter_context(tc.psum_pool(name="mm_psum", bufs=2))
         stat_psum = ctx.enter_context(tc.psum_pool(name="stat_psum", bufs=2))
@@ -76,10 +76,10 @@ def tile_mlstmblock_pb_t_kernel(tc, h_attn, gn_w, gn_b, W_out, x, skip_scale, ou
         gn_rows = consts.tile([P, P], BF16, name="gn_rows")
         nc.vector.memset(gn_rows[:], 0.0)
         tiles = CHANNELS // P
-        nc.sync.dma_start(out=gn_rows[0:tiles, :], in_=gn_w.rearrange("(c p) -> c p", p=P))
-        nc.sync.dma_start(out=gn_rows[tiles : 2 * tiles, :], in_=gn_b.rearrange("(c p) -> c p", p=P))
+        nc.scalar.dma_start(out=gn_rows[0:tiles, :], in_=gn_w.rearrange("(c p) -> c p", p=P))
+        nc.scalar.dma_start(out=gn_rows[tiles : 2 * tiles, :], in_=gn_b.rearrange("(c p) -> c p", p=P))
         skip_bf = consts.tile([P, 1], BF16, name="skip_bf")
-        nc.sync.dma_start(out=skip_bf[:], in_=skip_scale.partition_broadcast(P))
+        nc.scalar.dma_start(out=skip_bf[:], in_=skip_scale.partition_broadcast(P))
 
         load_h(0, 0, 0)
         load_h(0, 0, 1)
@@ -106,25 +106,22 @@ def tile_mlstmblock_pb_t_kernel(tc, h_attn, gn_w, gn_b, W_out, x, skip_scale, ou
         scale_bias = {}
 
         def start_stats(b, k):
-            for g in range(GROUPS_PER_PASS):
-                sq_parts[(b, k, g)] = stat_pool.tile([P, HALVES], F32, name="sq_part")
-            stat_banks[(b, k)] = stat_psum.tile([P, 16], F32, name="stat_bank")
+            sq_parts[(b, k)] = stat_pool.tile([P, GROUPS_PER_PASS, HALVES], F32, name="sq_part")
+            stat_banks[(b, k)] = stat_psum.tile([P, 32], F32, name="stat_bank")
 
         def square_sums(b, k, half):
             for g in range(GROUPS_PER_PASS):
                 squares = work.tile([P, HALF_ROWS, GROUP], BF16, name="squares")
-                src = h_tiles[(b, k, half)][:, :, g * GROUP : (g + 1) * GROUP]
-                part = sq_parts[(b, k, g)][:, half : half + 1]
-                if b == 0 and k == 0 and g == 1:
-                    nc.vector.scalar_tensor_tensor(
-                        out=squares[:], in0=src, scalar=1.0, in1=src, op0=ALU.mult, op1=ALU.mult, accum_out=part
-                    )
-                else:
-                    nc.scalar.activation(out=squares[:], in_=src, func=ACT.Square, accum_out=part)
+                nc.scalar.activation(
+                    out=squares[:],
+                    in_=h_tiles[(b, k, half)][:, :, g * GROUP : (g + 1) * GROUP],
+                    func=ACT.Square,
+                    accum_out=sq_parts[(b, k)][:, g, half : half + 1],
+                )
 
         def channel_sums(b, k, half):
-            for t in range(PACK):
-                col = t * HALVES + half
+            for t, copy in [(t, copy) for t in range(PACK) for copy in range(2)]:
+                col = t * HALVES + half + 16 * copy
                 for r in range(HALF_ROWS):
                     nc.tensor.matmul(
                         out=stat_banks[(b, k)][:, col : col + 1],
@@ -144,15 +141,10 @@ def tile_mlstmblock_pb_t_kernel(tc, h_attn, gn_w, gn_b, W_out, x, skip_scale, ou
             ex2 = bank[:, n_sum + GROUPS_PER_PASS : n_sum + 2 * GROUPS_PER_PASS]
             for j in range(per_group):
                 nc.tensor.matmul(out=mean, lhsT=mean_mat[:], rhs=sums[:, :, j], start=(j == 0), stop=(j == per_group - 1))
-            for g in range(GROUPS_PER_PASS):
-                for half in range(HALVES):
-                    nc.tensor.matmul(
-                        out=ex2[:, g : g + 1],
-                        lhsT=mean_mat[:],
-                        rhs=sq_parts[(b, k, g)][:, half : half + 1],
-                        start=(half == 0),
-                        stop=(half == HALVES - 1),
-                    )
+            for half in range(HALVES):
+                nc.tensor.matmul(
+                    out=ex2, lhsT=mean_mat[:], rhs=sq_parts[(b, k)][:, :, half], start=(half == 0), stop=(half == HALVES - 1)
+                )
             mean_sq = stat_pool.tile([P, GROUPS_PER_PASS], F32, name="mean_sq")
             nc.scalar.activation(out=mean_sq[:], in_=mean, func=ACT.Square)
             var_eps = stat_pool.tile([P, GROUPS_PER_PASS], F32, name="var_eps")

@@ -10,6 +10,7 @@ U32 = mybir.dt.uint32
 U8 = mybir.dt.uint8
 ALU = mybir.AluOpType
 ACT = mybir.ActivationFunctionType
+AXIS = mybir.AxisListType
 
 P = 128
 PACK = 4
@@ -22,10 +23,15 @@ EPS = 1e-5
 PASSES = CHANNELS // K_PASS
 GROUPS_PER_PASS = K_PASS // GROUP
 TILES_PER_GROUP = GROUP // P
+C_TILES = CHANNELS // P
 ROWS = SEQ // P
 HALVES = 2
 HALF_ROWS = ROWS // HALVES
 HALF_TOKENS = HALF_ROWS * P
+ROWS_PER_BANK = 2
+
+RESIDENT = 3
+UNITS_PER_BATCH = PASSES * HALVES
 
 FLOPS = 2 * BATCH * SEQ * CHANNELS * D_MODEL
 
@@ -38,14 +44,14 @@ def tile_mlstmblock_pb_t_kernel(tc, h_attn, gn_w, gn_b, W_out, x, skip_scale, ou
 
     with ExitStack() as ctx:
         consts = ctx.enter_context(tc.tile_pool(name="consts", bufs=1))
-        h_pool = ctx.enter_context(tc.tile_pool(name="h_pool", bufs=12))
+        h_pool = ctx.enter_context(tc.tile_pool(name="h_pool", bufs=RESIDENT * UNITS_PER_BATCH))
         x_pool = ctx.enter_context(tc.tile_pool(name="x_pool", bufs=3))
         work = ctx.enter_context(tc.tile_pool(name="work", bufs=2))
         codes_pool = ctx.enter_context(tc.tile_pool(name="codes_pool", bufs=1))
         stat_pool = ctx.enter_context(tc.tile_pool(name="stat_pool", bufs=3))
-        tp_psum = ctx.enter_context(tc.psum_pool(name="tp_psum", bufs=4))
+        tp_psum = ctx.enter_context(tc.psum_pool(name="tp_psum", bufs=PACK))
         mm_psum = ctx.enter_context(tc.psum_pool(name="mm_psum", bufs=2))
-        stat_psum = ctx.enter_context(tc.psum_pool(name="stat_psum", bufs=2))
+        stat_psum = ctx.enter_context(tc.psum_pool(name="stat_psum", bufs=PASSES))
 
         h_tiles = {}
         x_tiles = {}
@@ -75,9 +81,8 @@ def tile_mlstmblock_pb_t_kernel(tc, h_attn, gn_w, gn_b, W_out, x, skip_scale, ou
 
         gn_rows = consts.tile([P, P], BF16, name="gn_rows")
         nc.vector.memset(gn_rows[:], 0.0)
-        tiles = CHANNELS // P
-        nc.scalar.dma_start(out=gn_rows[0:tiles, :], in_=gn_w.rearrange("(c p) -> c p", p=P))
-        nc.scalar.dma_start(out=gn_rows[tiles : 2 * tiles, :], in_=gn_b.rearrange("(c p) -> c p", p=P))
+        nc.scalar.dma_start(out=gn_rows[0:C_TILES, :], in_=gn_w.rearrange("(c p) -> c p", p=P))
+        nc.scalar.dma_start(out=gn_rows[C_TILES : 2 * C_TILES, :], in_=gn_b.rearrange("(c p) -> c p", p=P))
         skip_bf = consts.tile([P, 1], BF16, name="skip_bf")
         nc.scalar.dma_start(out=skip_bf[:], in_=skip_scale.partition_broadcast(P))
 
@@ -89,25 +94,25 @@ def tile_mlstmblock_pb_t_kernel(tc, h_attn, gn_w, gn_b, W_out, x, skip_scale, ou
         load_h(0, 1, 1)
         load_x(0, 0)
         load_x(0, 1)
-        for b in (1, 2):
+        for b in range(1, RESIDENT):
             for k in range(PASSES):
                 for half in range(HALVES):
                     load_h(b, k, half)
 
-        gn_ps = tp_psum.tile([P, 8 * P], BF16, name="tp")
+        gn_ps = tp_psum.tile([P, HALF_TOKENS], BF16, name="tp")
         nc.tensor.transpose(gn_ps[:, 0:P], gn_rows[:], ident[:])
-        gn_cols = consts.tile([P, 2 * tiles], F32, name="gn_cols")
-        nc.vector.tensor_copy(out=gn_cols[:], in_=gn_ps[:, 0 : 2 * tiles])
+        gn_cols = consts.tile([P, 2 * C_TILES], F32, name="gn_cols")
+        nc.vector.tensor_copy(out=gn_cols[:], in_=gn_ps[:, 0 : 2 * C_TILES])
         skip_f = consts.tile([P, 1], F32, name="skip_f")
         nc.vector.tensor_copy(out=skip_f[:], in_=skip_bf[:])
 
-        sq_parts = {}
+        parts = {}
         stat_banks = {}
         scale_bias = {}
 
         def start_stats(b, k):
-            sq_parts[(b, k)] = stat_pool.tile([P, GROUPS_PER_PASS, HALVES], F32, name="sq_part")
-            stat_banks[(b, k)] = stat_psum.tile([P, 32], F32, name="stat_bank")
+            parts[(b, k)] = stat_pool.tile([P, 2, 8], F32, name="parts")
+            stat_banks[(b, k)] = stat_psum.tile([P, 16], F32, name="stat_bank")
 
         def square_sums(b, k, half):
             for g in range(GROUPS_PER_PASS):
@@ -116,12 +121,12 @@ def tile_mlstmblock_pb_t_kernel(tc, h_attn, gn_w, gn_b, W_out, x, skip_scale, ou
                     out=squares[:],
                     in_=h_tiles[(b, k, half)][:, :, g * GROUP : (g + 1) * GROUP],
                     func=ACT.Square,
-                    accum_out=sq_parts[(b, k)][:, g, half : half + 1],
+                    accum_out=parts[(b, k)][:, 1, g * HALVES + half : g * HALVES + half + 1],
                 )
 
         def channel_sums(b, k, half):
-            for t, copy in [(t, copy) for t in range(PACK) for copy in range(2)]:
-                col = t * HALVES + half + 16 * copy
+            for t in range(PACK):
+                col = t * HALVES + half
                 for r in range(HALF_ROWS):
                     nc.tensor.matmul(
                         out=stat_banks[(b, k)][:, col : col + 1],
@@ -134,17 +139,29 @@ def tile_mlstmblock_pb_t_kernel(tc, h_attn, gn_w, gn_b, W_out, x, skip_scale, ou
         def finish_stats(b, k):
             bank = stat_banks[(b, k)]
             n_sum = PACK * HALVES
-            per_group = n_sum // GROUPS_PER_PASS
-            sums = stat_pool.tile([P, GROUPS_PER_PASS, per_group], F32, name="sums")
-            nc.vector.tensor_copy(out=sums[:].rearrange("p g j -> p (g j)"), in_=bank[:, 0:n_sum])
-            mean = bank[:, n_sum : n_sum + GROUPS_PER_PASS]
-            ex2 = bank[:, n_sum + GROUPS_PER_PASS : n_sum + 2 * GROUPS_PER_PASS]
-            for j in range(per_group):
-                nc.tensor.matmul(out=mean, lhsT=mean_mat[:], rhs=sums[:, :, j], start=(j == 0), stop=(j == per_group - 1))
-            for half in range(HALVES):
-                nc.tensor.matmul(
-                    out=ex2, lhsT=mean_mat[:], rhs=sq_parts[(b, k)][:, :, half], start=(half == 0), stop=(half == HALVES - 1)
-                )
+            n_part = GROUPS_PER_PASS * HALVES
+            nc.vector.tensor_reduce(
+                out=parts[(b, k)][:, 0, 0:n_part].rearrange("p (g s) -> p g s", g=GROUPS_PER_PASS),
+                in_=bank[:, 0:n_sum].rearrange("p (g j s) -> p g s j", g=GROUPS_PER_PASS, j=TILES_PER_GROUP),
+                axis=AXIS.X,
+                op=ALU.add,
+            )
+            nc.tensor.matmul(
+                out=bank[:, n_sum : n_sum + 2 * n_part].rearrange("p (a c) -> p a c", a=2),
+                lhsT=mean_mat[:],
+                rhs=parts[(b, k)][:, :, 0:n_part],
+                start=True,
+                stop=True,
+            )
+            both = stat_pool.tile([P, 2, GROUPS_PER_PASS], F32, name="both")
+            nc.vector.tensor_reduce(
+                out=both[:],
+                in_=bank[:, n_sum : n_sum + 2 * n_part].rearrange("p (a g s) -> p a g s", a=2, g=GROUPS_PER_PASS),
+                axis=AXIS.X,
+                op=ALU.add,
+            )
+            mean = both[:, 0, :]
+            ex2 = both[:, 1, :]
             mean_sq = stat_pool.tile([P, GROUPS_PER_PASS], F32, name="mean_sq")
             nc.scalar.activation(out=mean_sq[:], in_=mean, func=ACT.Square)
             var_eps = stat_pool.tile([P, GROUPS_PER_PASS], F32, name="var_eps")
@@ -157,7 +174,7 @@ def tile_mlstmblock_pb_t_kernel(tc, h_attn, gn_w, gn_b, W_out, x, skip_scale, ou
             nc.vector.reciprocal(out=rstd[:], in_=std[:])
             shape = [P, GROUPS_PER_PASS, TILES_PER_GROUP]
             w_cols = gn_cols[:, k * PACK : (k + 1) * PACK].rearrange("p (g c) -> p g c", g=GROUPS_PER_PASS)
-            b_cols = gn_cols[:, tiles + k * PACK : tiles + (k + 1) * PACK].rearrange("p (g c) -> p g c", g=GROUPS_PER_PASS)
+            b_cols = gn_cols[:, C_TILES + k * PACK : C_TILES + (k + 1) * PACK].rearrange("p (g c) -> p g c", g=GROUPS_PER_PASS)
             scale = stat_pool.tile(shape, F32, name="scale")
             nc.vector.tensor_tensor(out=scale[:], in0=w_cols, in1=rstd[:].unsqueeze(2).to_broadcast(shape), op=ALU.mult)
             shift = stat_pool.tile(shape, F32, name="shift")
@@ -226,10 +243,10 @@ def tile_mlstmblock_pb_t_kernel(tc, h_attn, gn_w, gn_b, W_out, x, skip_scale, ou
 
         def project(b, half):
             result = work.tile([P, HALF_ROWS, D_MODEL], F32, name="result")
-            for pair in range(HALF_ROWS // 2):
-                acc = mm_psum.tile([P, 2, D_MODEL], F32, name="acc")
-                for s in range(2):
-                    r = 2 * pair + s
+            for pair in range(HALF_ROWS // ROWS_PER_BANK):
+                acc = mm_psum.tile([P, ROWS_PER_BANK, D_MODEL], F32, name="acc")
+                for s in range(ROWS_PER_BANK):
+                    r = ROWS_PER_BANK * pair + s
                     for k in range(PASSES):
                         codes, scales = h_codes[(k, half)]
                         nc.tensor.matmul_mx(
@@ -241,9 +258,10 @@ def tile_mlstmblock_pb_t_kernel(tc, h_attn, gn_w, gn_b, W_out, x, skip_scale, ou
                             start=(k == 0),
                             stop=(k == PASSES - 1),
                         )
+                rows = slice(ROWS_PER_BANK * pair, ROWS_PER_BANK * (pair + 1))
                 nc.vector.scalar_tensor_tensor(
-                    out=result[:, 2 * pair : 2 * pair + 2, :].rearrange("p s d -> p (s d)"),
-                    in0=x_tiles[(b, half)][:, 2 * pair : 2 * pair + 2, :].rearrange("p s d -> p (s d)"),
+                    out=result[:, rows, :].rearrange("p s d -> p (s d)"),
+                    in0=x_tiles[(b, half)][:, rows, :].rearrange("p s d -> p (s d)"),
                     scalar=skip_f[:, 0:1],
                     in1=acc[:].rearrange("p s d -> p (s d)"),
                     op0=ALU.mult,
@@ -274,7 +292,7 @@ def tile_mlstmblock_pb_t_kernel(tc, h_attn, gn_w, gn_b, W_out, x, skip_scale, ou
                         finish_stats(b + 1, k)
                     if k == PASSES - 1:
                         project(b, half)
-                    if b + 3 < BATCH:
-                        load_h(b + 3, k, half)
+                    if b + RESIDENT < BATCH:
+                        load_h(b + RESIDENT, k, half)
                     if b + 1 < BATCH and k == 0:
                         load_x(b + 1, half)

from contextlib import ExitStack

import concourse.mybir as mybir
from concourse.masks import make_identity

FP8X4 = mybir.dt.float8_e4m3fn_x4
BF16 = mybir.dt.bfloat16
F32 = mybir.dt.float32
U32 = mybir.dt.uint32
U8 = mybir.dt.uint8
ALU = mybir.AluOpType
ACT = mybir.ActivationFunctionType
AXIS = mybir.AxisListType

P = 128
PACK = 4
K_PASS = P * PACK

BATCH, SEQ, CHANNELS, D_MODEL = 4, 2048, 1024, 256
GROUP = 256
EPS = 1e-5

PASSES = CHANNELS // K_PASS
GROUPS_PER_PASS = K_PASS // GROUP
TILES_PER_GROUP = GROUP // P
C_TILES = CHANNELS // P
ROWS = SEQ // P
HALVES = 2
HALF_ROWS = ROWS // HALVES
HALF_TOKENS = HALF_ROWS * P
ROWS_PER_BANK = 2

RESIDENT = 3
UNITS_PER_BATCH = PASSES * HALVES

FLOPS = 2 * BATCH * SEQ * CHANNELS * D_MODEL


def tile_mlstmblock_pb_t_kernel(tc, h_attn, gn_w, gn_b, W_out, x, skip_scale, out):
    nc = tc.nc
    h_view = h_attn.rearrange("b (p r) c -> b p r c", r=ROWS)
    x_view = x.rearrange("b (p r) d -> b p r d", r=ROWS)
    out_view = out.rearrange("b (p r) d -> b p r d", r=ROWS)

    with ExitStack() as ctx:
        consts = ctx.enter_context(tc.tile_pool(name="consts", bufs=1))
        h_pool = ctx.enter_context(tc.tile_pool(name="h_pool", bufs=RESIDENT * UNITS_PER_BATCH))
        x_pool = ctx.enter_context(tc.tile_pool(name="x_pool", bufs=3))
        work = ctx.enter_context(tc.tile_pool(name="work", bufs=2))
        codes_pool = ctx.enter_context(tc.tile_pool(name="codes_pool", bufs=1))
        stat_pool = ctx.enter_context(tc.tile_pool(name="stat_pool", bufs=3))
        tp_psum = ctx.enter_context(tc.psum_pool(name="tp_psum", bufs=PACK))
        mm_psum = ctx.enter_context(tc.psum_pool(name="mm_psum", bufs=2))
        stat_psum = ctx.enter_context(tc.psum_pool(name="stat_psum", bufs=PASSES))

        h_tiles = {}
        x_tiles = {}

        def load_h(b, k, half):
            h_tile = h_pool.tile([P, HALF_ROWS, K_PASS], BF16, name="h_tile")
            nc.sync.dma_start(
                out=h_tile[:],
                in_=h_view[b, :, half * HALF_ROWS : (half + 1) * HALF_ROWS, k * K_PASS : (k + 1) * K_PASS],
            )
            h_tiles[(b, k, half)] = h_tile

        def load_x(b, half):
            x_tile = x_pool.tile([P, HALF_ROWS, D_MODEL], BF16, name="x_tile")
            nc.sync.dma_start(out=x_tile[:], in_=x_view[b, :, half * HALF_ROWS : (half + 1) * HALF_ROWS, :])
            x_tiles[(b, half)] = x_tile

        ident = consts.tile([P, P], BF16, name="ident")
        make_identity(nc, ident[:])
        ones_col = consts.tile([P, 2], BF16, name="ones_col")
        nc.vector.memset(ones_col[:], 1.0)
        mean_mat = consts.tile([P, P], F32, name="mean_mat")
        nc.vector.memset(mean_mat[:], 1.0 / (SEQ * GROUP))
        warm = consts.tile([P, 1], F32, name="warm")
        nc.vector.memset(warm[:], 1.0)
        nc.scalar.activation(out=warm[:], in_=warm[:], func=ACT.Sqrt)

        gn_rows = consts.tile([P, P], BF16, name="gn_rows")
        nc.vector.memset(gn_rows[:], 0.0)
        nc.scalar.dma_start(out=gn_rows[0:C_TILES, :], in_=gn_w.rearrange("(c p) -> c p", p=P))
        nc.scalar.dma_start(out=gn_rows[C_TILES : 2 * C_TILES, :], in_=gn_b.rearrange("(c p) -> c p", p=P))
        skip_bf = consts.tile([P, 1], BF16, name="skip_bf")
        nc.scalar.dma_start(out=skip_bf[:], in_=skip_scale.partition_broadcast(P))

        load_h(0, 0, 0)
        load_h(0, 0, 1)
        w_raw = consts.tile([P, D_MODEL // P, CHANNELS], BF16, name="w_raw")
        nc.sync.dma_start(out=w_raw[:], in_=W_out.rearrange("(m p) c -> p m c", p=P))
        load_h(0, 1, 0)
        load_h(0, 1, 1)
        load_x(0, 0)
        load_x(0, 1)
        for b in range(1, RESIDENT):
            for k in range(PASSES):
                for half in range(HALVES):
                    load_h(b, k, half)

        gn_ps = tp_psum.tile([P, HALF_TOKENS], BF16, name="tp")
        nc.tensor.transpose(gn_ps[:, 0:P], gn_rows[:], ident[:])
        gn_cols = consts.tile([P, 2 * C_TILES], F32, name="gn_cols")
        nc.vector.tensor_copy(out=gn_cols[:], in_=gn_ps[:, 0 : 2 * C_TILES])
        skip_f = consts.tile([P, 1], F32, name="skip_f")
        nc.vector.tensor_copy(out=skip_f[:], in_=skip_bf[:])

        parts = {}
        stat_banks = {}
        scale_bias = {}

        def start_stats(b, k):
            parts[(b, k)] = stat_pool.tile([P, 2, 8], F32, name="parts")
            stat_banks[(b, k)] = stat_psum.tile([P, 16], F32, name="stat_bank")

        def square_sums(b, k, half):
            for g in range(GROUPS_PER_PASS):
                squares = work.tile([P, HALF_ROWS, GROUP], BF16, name="squares")
                nc.scalar.activation(
                    out=squares[:],
                    in_=h_tiles[(b, k, half)][:, :, g * GROUP : (g + 1) * GROUP],
                    func=ACT.Square,
                    accum_out=parts[(b, k)][:, 1, g * HALVES + half : g * HALVES + half + 1],
                )

        def channel_sums(b, k, half):
            for t in range(PACK):
                col = t * HALVES + half
                for r in range(HALF_ROWS):
                    nc.tensor.matmul(
                        out=stat_banks[(b, k)][:, col : col + 1],
                        lhsT=h_tiles[(b, k, half)][:, r, t * P : (t + 1) * P],
                        rhs=ones_col[:, 0:1],
                        start=(r == 0),
                        stop=(r == HALF_ROWS - 1),
                    )

        def finish_stats(b, k):
            bank = stat_banks[(b, k)]
            n_sum = PACK * HALVES
            n_part = GROUPS_PER_PASS * HALVES
            nc.vector.tensor_reduce(
                out=parts[(b, k)][:, 0, 0:n_part].rearrange("p (g s) -> p g s", g=GROUPS_PER_PASS),
                in_=bank[:, 0:n_sum].rearrange("p (g j s) -> p g s j", g=GROUPS_PER_PASS, j=TILES_PER_GROUP),
                axis=AXIS.X,
                op=ALU.add,
            )
            nc.tensor.matmul(
                out=bank[:, n_sum : n_sum + 2 * n_part].rearrange("p (a c) -> p a c", a=2),
                lhsT=mean_mat[:],
                rhs=parts[(b, k)][:, :, 0:n_part],
                start=True,
                stop=True,
            )
            both = stat_pool.tile([P, 2, GROUPS_PER_PASS], F32, name="both")
            nc.vector.tensor_reduce(
                out=both[:],
                in_=bank[:, n_sum : n_sum + 2 * n_part].rearrange("p (a g s) -> p a g s", a=2, g=GROUPS_PER_PASS),
                axis=AXIS.X,
                op=ALU.add,
            )
            mean = both[:, 0, :]
            ex2 = both[:, 1, :]
            mean_sq = stat_pool.tile([P, GROUPS_PER_PASS], F32, name="mean_sq")
            nc.scalar.activation(out=mean_sq[:], in_=mean, func=ACT.Square)
            var_eps = stat_pool.tile([P, GROUPS_PER_PASS], F32, name="var_eps")
            nc.vector.scalar_tensor_tensor(
                out=var_eps[:], in0=ex2, scalar=EPS, in1=mean_sq[:], op0=ALU.add, op1=ALU.subtract
            )
            std = stat_pool.tile([P, GROUPS_PER_PASS], F32, name="std")
            nc.scalar.activation(out=std[:], in_=var_eps[:], func=ACT.Sqrt)
            rstd = stat_pool.tile([P, GROUPS_PER_PASS], F32, name="rstd")
            nc.vector.reciprocal(out=rstd[:], in_=std[:])
            shape = [P, GROUPS_PER_PASS, TILES_PER_GROUP]
            w_cols = gn_cols[:, k * PACK : (k + 1) * PACK].rearrange("p (g c) -> p g c", g=GROUPS_PER_PASS)
            b_cols = gn_cols[:, C_TILES + k * PACK : C_TILES + (k + 1) * PACK].rearrange("p (g c) -> p g c", g=GROUPS_PER_PASS)
            scale = stat_pool.tile(shape, F32, name="scale")
            nc.vector.tensor_tensor(out=scale[:], in0=w_cols, in1=rstd[:].unsqueeze(2).to_broadcast(shape), op=ALU.mult)
            shift = stat_pool.tile(shape, F32, name="shift")
            nc.vector.tensor_tensor(out=shift[:], in0=scale[:], in1=mean.unsqueeze(2).to_broadcast(shape), op=ALU.mult)
            bias = stat_pool.tile(shape, F32, name="bias")
            nc.vector.tensor_tensor(out=bias[:], in0=b_cols, in1=shift[:], op=ALU.subtract)
            scale_bias[(b, k)] = (scale[:].rearrange("p g c -> p (g c)"), bias[:].rearrange("p g c -> p (g c)"))

        w_grouped = consts.tile([P, PASSES, D_MODEL, PACK], BF16, name="w_grouped", align_bytes=64)
        w_codes = consts.tile([P, PASSES * D_MODEL], U32, name="w_codes", align_bytes=64)
        w_scales = consts.tile([P, PASSES * D_MODEL], U8, name="w_scales", align_bytes=64)

        def prepare_w():
            for k in range(PASSES):
                w_ps = tp_psum.tile([P, PACK * D_MODEL], BF16, name="tp")
                for t in range(PACK):
                    for m in range(D_MODEL // P):
                        c0 = k * K_PASS + t * P
                        nc.tensor.transpose(
                            w_ps[:, t * D_MODEL + m * P : t * D_MODEL + (m + 1) * P], w_raw[:, m, c0 : c0 + P], ident[:]
                        )
                nc.vector.tensor_copy(out=w_grouped[:, k], in_=w_ps[:].rearrange("p (t n) -> p n t", t=PACK))
            nc.vector.quantize_mx(
                out=w_codes[:].bitcast(FP8X4),
                scales=w_scales[:],
                in_=w_grouped[:].rearrange("p k n t -> p (k n t)"),
            )

        h_codes = {}

        def normalise(b, k, half):
            scale, bias = scale_bias[(b, k)]
            planes = work.tile([P, PACK, HALF_TOKENS], BF16, name="planes")
            on_scalar = 1 + half
            for t in range(PACK):
                tp = tp_psum.tile([P, HALF_TOKENS], BF16, name="tp")
                for r in range(HALF_ROWS):
                    nc.tensor.transpose(tp[:, r * P : (r + 1) * P], h_tiles[(b, k, half)][:, r, t * P : (t + 1) * P], ident[:])
                if t >= PACK - on_scalar:
                    nc.scalar.activation(
                        out=planes[:, t, :], in_=tp[:], func=ACT.Identity, scale=scale[:, t : t + 1], bias=bias[:, t : t + 1]
                    )
                else:
                    nc.vector.tensor_scalar(
                        out=planes[:, t, :],
                        in0=tp[:],
                        scalar1=scale[:, t : t + 1],
                        scalar2=bias[:, t : t + 1],
                        op0=ALU.mult,
                        op1=ALU.add,
                    )
            return planes

        def quantise(b, k, half, planes):
            grouped = work.tile([P, HALF_TOKENS, PACK], BF16, name="grouped", align_bytes=64)
            nc.vector.tensor_copy(
                out=grouped[:].rearrange("p (c i) t -> p c t i", i=4),
                in_=planes[:].rearrange("p t (c i) -> p c t i", i=4),
            )
            codes = codes_pool.tile([P, HALF_TOKENS], U32, name="codes%d%d" % (k, half), align_bytes=64)
            scales = codes_pool.tile([P, HALF_TOKENS], U8, name="scales%d%d" % (k, half), align_bytes=64)
            nc.vector.quantize_mx(
                out=codes[:].bitcast(FP8X4), scales=scales[:], in_=grouped[:].rearrange("p r t -> p (r t)")
            )
            h_codes[(k, half)] = (codes, scales)

        def project(b, half):
            result = work.tile([P, HALF_ROWS, D_MODEL], F32, name="result")
            for pair in range(HALF_ROWS // ROWS_PER_BANK):
                acc = mm_psum.tile([P, ROWS_PER_BANK, D_MODEL], F32, name="acc")
                for s in range(ROWS_PER_BANK):
                    r = ROWS_PER_BANK * pair + s
                    for k in range(PASSES):
                        codes, scales = h_codes[(k, half)]
                        nc.tensor.matmul_mx(
                            out=acc[:, s, :],
                            lhsT=codes[:, r * P : (r + 1) * P].bitcast(FP8X4),
                            lhsT_scale=scales[:, r * P : (r + 1) * P],
                            rhs=w_codes[:, k * D_MODEL : (k + 1) * D_MODEL].bitcast(FP8X4),
                            rhs_scale=w_scales[:, k * D_MODEL : (k + 1) * D_MODEL],
                            start=(k == 0),
                            stop=(k == PASSES - 1),
                        )
                rows = slice(ROWS_PER_BANK * pair, ROWS_PER_BANK * (pair + 1))
                nc.vector.scalar_tensor_tensor(
                    out=result[:, rows, :].rearrange("p s d -> p (s d)"),
                    in0=x_tiles[(b, half)][:, rows, :].rearrange("p s d -> p (s d)"),
                    scalar=skip_f[:, 0:1],
                    in1=acc[:].rearrange("p s d -> p (s d)"),
                    op0=ALU.mult,
                    op1=ALU.add,
                )
            nc.sync.dma_start(out=out_view[b, :, half * HALF_ROWS : (half + 1) * HALF_ROWS, :], in_=result[:])

        for k in range(PASSES):
            start_stats(0, k)
            for half in range(HALVES):
                square_sums(0, k, half)
                channel_sums(0, k, half)
            finish_stats(0, k)
            if k == 0:
                prepare_w()

        for b in range(BATCH):
            for k in range(PASSES):
                for half in range(HALVES):
                    planes = normalise(b, k, half)
                    if b + 1 < BATCH:
                        if half == 0:
                            start_stats(b + 1, k)
                        square_sums(b + 1, k, half)
                        channel_sums(b + 1, k, half)
                    quantise(b, k, half, planes)
                    if b + 1 < BATCH and half == HALVES - 1:
                        finish_stats(b + 1, k)
                    if k == PASSES - 1:
                        project(b, half)
                    if b + RESIDENT < BATCH:
                        load_h(b + RESIDENT, k, half)
                    if b + 1 < BATCH and k == 0:
                        load_x(b + 1, half)
